import numpy as np
import ml_dtypes


def mxq(x, axis, fmt="e4m3"):
    dtype, down = {"e4m3": (ml_dtypes.float8_e4m3fn, 7), "e5m2": (ml_dtypes.float8_e5m2, 14)}[fmt]
    v = np.moveaxis(np.asarray(x, np.float32).astype(ml_dtypes.bfloat16).astype(np.float64), axis, -1)
    blocks = v.reshape(v.shape[:-1] + (-1, 32))
    amax = np.abs(blocks).max(-1, keepdims=True)
    byte = np.maximum(np.where(amax > 0, np.frexp(amax)[1] - 1 + 127, 0) - down, 1)
    scale = np.exp2(byte - 127.0)
    codes = (blocks / scale).astype(np.float32).astype(dtype).astype(np.float64)
    return np.moveaxis((codes * scale).reshape(v.shape), -1, axis)


WIDE = False


def mx_kscale(k):
    if not WIDE:
        return np.ones(k)
    levels = np.array([10, -10, 5, -5, 0])
    a = np.random.permutation(np.resize(levels, k // 512 * 4)).reshape(k // 512, 4)
    idx = np.arange(k)
    return np.exp2(a[idx // 512, idx % 128 // 32])


BF16 = ml_dtypes.bfloat16


def bf(x):
    return np.asarray(x, np.float32).astype(BF16)


def f64(x):
    return np.asarray(x).astype(np.float64)


B, T, E, Q = 4, 256, 512, 128
EPS_RMS = 1.1920929e-07


def silu(t):
    return t * (1.0 / (1.0 + np.exp(-t)))


def rms_norm(t):
    return t * (1.0 / np.sqrt(np.mean(t * t, axis=-1, keepdims=True) + EPS_RMS))


def w_norm(w, n):
    target_std = n ** (-0.5)
    return w * (target_std / (np.std(w, ddof=1) + 1e-08))


def setup_inputs():
    s = mx_kscale(E)
    u = s / s.min()
    row = np.where(u > 1.0, np.sqrt(EPS_RMS) / u, np.sqrt(T / (B * E)) * np.exp2(np.random.uniform(-1.0, 1.0, E)))
    return {"ao": bf(np.random.standard_normal((E, E)) * row[:, None]),
            "w_qkv": bf(np.random.standard_normal((3 * Q, E)) / np.sqrt(E) * u),
            "out_w": bf((np.random.standard_normal((E, E)) * np.sqrt(E) + 2.0) / E * u[:, None]),
            "tao": bf(np.random.uniform(0.5, 1.5, 1) * np.random.choice([-1.0, 1.0], 1))}


def reference(ao, w_qkv, out_w, tao):
    w = f64(w_qkv)
    alpha = np.clip(np.abs(f64(tao)), 1e-08, 1.0)
    ao_n = rms_norm(f64(ao))
    n1 = silu(mxq(w, 1, "e4m3") @ mxq(ao_n, 0, "e4m3"))
    upd = mxq(n1, 1, "e4m3") @ mxq(f64(out_w).T, 0, "e4m3")
    return w_norm(w + upd, E) * alpha

@@ -1,0 +1,235 @@
+from contextlib import ExitStack
+import math
+
+import concourse.mybir as mybir
+from concourse.masks import make_identity
+
+F32 = mybir.dt.float32
+BF16 = mybir.dt.bfloat16
+U32 = mybir.dt.uint32
+U8 = mybir.dt.uint8
+FP8X4 = mybir.dt.float8_e4m3fn_x4
+ACT = mybir.ActivationFunctionType
+ALU = mybir.AluOpType
+
+P = 128
+PACK = 4
+K = P * PACK
+W_TILES = 3
+OW_TILES = 4
+COUNT = W_TILES * P * K
+EPS_RMS = 1.1920929e-07
+EPS_STD = 1e-08
+
+FLOPS = 2 * 2 * W_TILES * P * K * K
+
+
+def transpose_words(nc, flip, ident, rows_sb, first, count):
+    flipped = flip.tile([P, 2, 2, P], F32, tag="flip")
+    for r in range(count):
+        words = rows_sb[:, first + r, :].bitcast(F32)
+        for u in range(2):
+            nc.tensor.transpose(flipped[:, r, u, :], words[:, u * P : (u + 1) * P], ident[:])
+    return flipped
+
+
+def grouped_views(grouped, flipped, first, count):
+    dst = grouped[:, first * P : (first + count) * P, :].rearrange("p (r i) u -> p r i u", r=count)
+    src = flipped[:, 0:count].rearrange("p r u i -> p r i u")
+    return dst, src
+
+
+def quantise(nc, codes, scales, grouped_bf16, first_col, cols):
+    nc.vector.quantize_mx(
+        out=codes[:, first_col : first_col + cols].bitcast(FP8X4),
+        scales=scales[:, first_col : first_col + cols],
+        in_=grouped_bf16[:, first_col * PACK : (first_col + cols) * PACK],
+    )
+
+
+def tile_retentionmechanism_pb_s_kernel(tc, ao, w_qkv, out_w, tao, out):
+    nc = tc.nc
+    with ExitStack() as ctx:
+        keep = ctx.enter_context(tc.tile_pool(name="keep", bufs=1))
+        flip = ctx.enter_context(tc.psum_pool(name="flip", bufs=4))
+        acc = ctx.enter_context(tc.psum_pool(name="acc", bufs=3))
+
+        ao_sb = keep.tile([P, PACK, K], BF16)
+        ao_rows = ao.rearrange("(u p h) e -> u p h e", u=2, h=2)
+        for u in range(2):
+            nc.sync.dma_start(out=ao_sb[:, 2 * u : 2 * u + 2, :], in_=ao_rows[u])
+        w_sb = keep.tile([P, W_TILES, K], BF16)
+        nc.sync.dma_start(out=w_sb[:], in_=w_qkv.rearrange("(r p) d -> p r d", p=P))
+        ow_sb = keep.tile([P, OW_TILES, K], BF16)
+        nc.sync.dma_start(out=ow_sb[:], in_=out_w.rearrange("(r p) e -> p r e", p=P))
+        tao_sb = keep.tile([P, 1], BF16)
+        nc.scalar.dma_start(out=tao_sb[:], in_=tao.partition_broadcast(P))
+
+        ident = keep.tile([P, P], F32)
+        make_identity(nc, ident[:])
+        ones = keep.tile([P, P], F32)
+        nc.gpsimd.memset(ones[:], 1.0)
+        half = keep.tile([P, 1], F32)
+        nc.gpsimd.memset(half[:], 0.5)
+        one = keep.tile([P, 1], F32)
+        nc.vector.memset(one[:], 1.0)
+        eps_rms = keep.tile([P, 1], F32)
+        nc.vector.tensor_scalar(
+            out=eps_rms[:], in0=one[:], scalar1=0.0, scalar2=EPS_RMS, op0=ALU.mult, op1=ALU.add
+        )
+        unread = keep.tile([P, 2, 8], F32)
+        nc.scalar.activation(out=unread[:, 0, 0:1], in_=one[:], func=ACT.Sqrt)
+
+        squares = keep.tile([P, PACK, K], F32)
+        sumsq = keep.tile([P, 2, 8], F32)
+        for u in range(2):
+            nc.scalar.activation(
+                out=squares[:, 2 * u, :], in_=ao_sb[:, 2 * u, :], func=ACT.Square,
+                accum_out=sumsq[:, 0, u : u + 1],
+            )
+            nc.vector.scalar_tensor_tensor(
+                out=squares[:, 2 * u + 1, :], in0=ao_sb[:, 2 * u + 1, :], scalar=1.0,
+                in1=ao_sb[:, 2 * u + 1, :], op0=ALU.mult, op1=ALU.mult,
+                accum_out=sumsq[:, 1, u : u + 1],
+            )
+        rms = keep.tile([P, PACK], F32)
+        nc.scalar.activation(
+            out=rms[:].rearrange("p (u h) -> p h u", h=2), in_=sumsq[:, :, 0:2], func=ACT.Sqrt,
+            bias=eps_rms[:], scale=1.0 / K,
+        )
+        rstd = keep.tile([P, PACK], F32)
+        nc.vector.reciprocal(out=rstd[:], in_=rms[:])
+
+        w_flipped = [transpose_words(nc, flip, ident, w_sb, 0, 2), transpose_words(nc, flip, ident, w_sb, 2, 1)]
+        ow_flipped = [transpose_words(nc, flip, ident, ow_sb, 0, 2), transpose_words(nc, flip, ident, ow_sb, 2, 2)]
+
+        w_grouped = keep.tile([P, W_TILES * P, 2], F32, align_bytes=64)
+        dst, src = grouped_views(w_grouped, w_flipped[0], 0, 2)
+        nc.scalar.copy(out=dst, in_=src)
+        dst, src = grouped_views(w_grouped, w_flipped[1], 2, 1)
+        nc.scalar.copy(out=dst, in_=src)
+        nc.scalar.activation(out=unread[:, 1, 0:1], in_=rms[:, 0:1], func=ACT.Silu)
+        ow_grouped = keep.tile([P, OW_TILES * P, 2], F32, align_bytes=64)
+        dst, src = grouped_views(ow_grouped, ow_flipped[0], 0, 2)
+        nc.scalar.copy(out=dst, in_=src)
+
+        a_grouped = keep.tile([P, PACK, P, PACK], BF16, align_bytes=64)
+        a_flat = a_grouped[:].rearrange("p e m t -> p (e m t)")
+        a_codes = keep.tile([P, K], U32, align_bytes=64)
+        a_scales = keep.tile([P, K], U8, align_bytes=64)
+        w_codes = keep.tile([P, W_TILES * P], U32, align_bytes=64)
+        w_scales = keep.tile([P, W_TILES * P], U8, align_bytes=64)
+        w_flat = w_grouped[:].rearrange("p i u -> p (i u)").bitcast(BF16)
+        ao_cols = ao_sb[:].rearrange("p t (u m h) -> p u h m t", u=2, h=2)
+        rstd_all = rstd[:].unsqueeze(1).to_broadcast([P, P, PACK])
+        n_ps = [acc.tile([P, PACK, P], F32, tag="acc", name="n_ps%d" % r) for r in range(W_TILES)]
+        for u in range(2):
+            for h in range(2):
+                nc.vector.tensor_tensor(
+                    out=a_grouped[:, 2 * u + h], in0=ao_cols[:, u, h], in1=rstd_all, op=ALU.mult
+                )
+            if u == 0:
+                quantise(nc, w_codes, w_scales, w_flat, 0, 2 * P)
+                quantise(nc, w_codes, w_scales, w_flat, 2 * P, P)
+            quantise(nc, a_codes, a_scales, a_flat, 2 * u * P, 2 * P)
+            for r in range(W_TILES):
+                for e_tile in (2 * u, 2 * u + 1):
+                    nc.tensor.matmul_mx(
+                        out=n_ps[r][:, e_tile, :],
+                        lhsT=a_codes[:, e_tile * P : (e_tile + 1) * P].bitcast(FP8X4),
+                        lhsT_scale=a_scales[:, e_tile * P : (e_tile + 1) * P],
+                        rhs=w_codes[:, r * P : (r + 1) * P].bitcast(FP8X4),
+                        rhs_scale=w_scales[:, r * P : (r + 1) * P],
+                        start=True,
+                        stop=True,
+                    )
+
+        dst, src = grouped_views(ow_grouped, ow_flipped[1], 2, 2)
+        nc.vector.tensor_copy(out=dst, in_=src)
+        ow_codes = keep.tile([P, K], U32, align_bytes=64)
+        ow_scales = keep.tile([P, K], U8, align_bytes=64)
+        quantise(nc, ow_codes, ow_scales, ow_grouped[:].rearrange("p j u -> p (j u)").bitcast(BF16), 0, K)
+
+        gate = keep.tile([P, 1], F32)
+        nc.vector.scalar_tensor_tensor(
+            out=gate[:], in0=tao_sb[:], scalar=-1.0, in1=tao_sb[:], op0=ALU.mult, op1=ALU.max
+        )
+        clipped = keep.tile([P, 1], F32)
+        nc.vector.tensor_scalar(
+            out=clipped[:], in0=gate[:], scalar1=1e-08, scalar2=1.0, op0=ALU.max, op1=ALU.min
+        )
+        scaled_gate = keep.tile([P, 1], F32)
+        nc.vector.tensor_scalar(
+            out=scaled_gate[:], in0=clipped[:], scalar1=math.sqrt((COUNT - 1) / K), scalar2=None, op0=ALU.mult
+        )
+        gate_inv = keep.tile([P, 1], F32)
+        nc.vector.reciprocal(out=gate_inv[:], in_=scaled_gate[:])
+
+        n_grouped = keep.tile([P, W_TILES, P, PACK], BF16, align_bytes=64)
+        n_flat = n_grouped[:].rearrange("p r i t -> p (r i t)")
+        n_codes = keep.tile([P, W_TILES * P], U32, align_bytes=64)
+        n_scales = keep.tile([P, W_TILES * P], U8, align_bytes=64)
+        z_sb = keep.tile([P, W_TILES, K], F32)
+        z_squares = keep.tile([P, W_TILES, K], F32)
+        sum_z = keep.tile([P, W_TILES], F32)
+        sum_zz = keep.tile([P, W_TILES], F32)
+        total_z = flip.tile([P, 1], F32, tag="flip")
+        total_zz = flip.tile([P, 1], F32, tag="flip")
+        for r in range(W_TILES):
+            nc.scalar.activation(
+                out=n_grouped[:, r], in_=n_ps[r][:].rearrange("p t i -> p i t"), func=ACT.Silu
+            )
+            quantise(nc, n_codes, n_scales, n_flat, r * P, P)
+            z_ps = acc.tile([P, K], F32, tag="acc")
+            nc.tensor.matmul_mx(
+                out=z_ps[:],
+                lhsT=n_codes[:, r * P : (r + 1) * P].bitcast(FP8X4),
+                lhsT_scale=n_scales[:, r * P : (r + 1) * P],
+                rhs=ow_codes[:].bitcast(FP8X4),
+                rhs_scale=ow_scales[:],
+                start=True,
+                stop=True,
+            )
+            nc.vector.scalar_tensor_tensor(
+                out=z_sb[:, r, :], in0=z_ps[:], scalar=1.0, in1=w_sb[:, r, :], op0=ALU.mult, op1=ALU.add,
+                accum_out=sum_z[:, r : r + 1],
+            )
+            nc.scalar.activation(
+                out=z_squares[:, r, :], in_=z_sb[:, r, :], func=ACT.Square, accum_out=sum_zz[:, r : r + 1]
+            )
+            nc.tensor.matmul(
+                out=total_z[:], lhsT=ones[:], rhs=sum_z[:, r : r + 1], start=(r == 0), stop=(r == W_TILES - 1)
+            )
+            nc.tensor.matmul(
+                out=total_zz[:], lhsT=ones[:], rhs=sum_zz[:, r : r + 1], start=(r == 0), stop=(r == W_TILES - 1)
+            )
+
+        minus_mean_part = keep.tile([P, 1], F32)
+        nc.vector.tensor_scalar(
+            out=minus_mean_part[:], in0=total_z[:], scalar1=total_z[:, 0:1], scalar2=-1.0 / COUNT,
+            op0=ALU.mult, op1=ALU.mult,
+        )
+        spread = keep.tile([P, 1], F32)
+        nc.vector.tensor_scalar(
+            out=spread[:], in0=total_zz[:], scalar1=minus_mean_part[:, 0:1], scalar2=0.0, op0=ALU.add, op1=ALU.max
+        )
+        root = keep.tile([P, 1], F32)
+        nc.gpsimd.tensor_tensor(out=root[:], in0=spread[:], in1=half[:], op=ALU.pow)
+        divisor = keep.tile([P, 1], F32)
+        nc.vector.tensor_scalar(
+            out=divisor[:], in0=root[:], scalar1=EPS_STD * math.sqrt(COUNT - 1), scalar2=gate_inv[:, 0:1],
+            op0=ALU.add, op1=ALU.mult,
+        )
+        factor = keep.tile([P, 1], F32)
+        nc.vector.reciprocal(out=factor[:], in_=divisor[:])
+
+        result = keep.tile([P, W_TILES, K], F32)
+        out_tiles = out.rearrange("(r p) j -> r p j", p=P)
+        for r in range(W_TILES):
+            if r == 1:
+                nc.scalar.activation(out=result[:, r, :], in_=z_sb[:, r, :], func=ACT.Copy, scale=factor[:, 0:1])
+            else:
+                nc.vector.tensor_scalar(
+                    out=result[:, r, :], in0=z_sb[:, r, :], scalar1=factor[:, 0:1], scalar2=None, op0=ALU.mult
+                )
+            nc.sync.dma_start(out=out_tiles[r], in_=result[:, r, :])

@@ -53,6 +53,7 @@ def tile_retentionmechanism_pb_s_kernel(tc, ao, w_qkv, out_w, tao, out):
         keep = ctx.enter_context(tc.tile_pool(name="keep", bufs=1))
         flip = ctx.enter_context(tc.psum_pool(name="flip", bufs=4))
         acc = ctx.enter_context(tc.psum_pool(name="acc", bufs=3))
+        ctx.enter_context(tc.manual_schedule())
 
         ao_sb = keep.tile([P, PACK, K], BF16)
         ao_rows = ao.rearrange("(u p h) e -> u p h e", u=2, h=2)
@@ -175,14 +176,16 @@ def tile_retentionmechanism_pb_s_kernel(tc, ao, w_qkv, out_w, tao, out):
         sum_zz = keep.tile([P, W_TILES], F32)
         total_z = flip.tile([P, 1], F32, tag="flip")
         total_zz = flip.tile([P, 1], F32, tag="flip")
-        for r in range(W_TILES):
+        z_ps = [None] * W_TILES
+
+        def silu_quantise_multiply(r):
             nc.scalar.activation(
                 out=n_grouped[:, r], in_=n_ps[r][:].rearrange("p t i -> p i t"), func=ACT.Silu
             )
             quantise(nc, n_codes, n_scales, n_flat, r * P, P)
-            z_ps = acc.tile([P, K], F32, tag="acc")
+            z_ps[r] = acc.tile([P, K], F32, tag="acc", name="z_ps%d" % r)
             nc.tensor.matmul_mx(
-                out=z_ps[:],
+                out=z_ps[r][:],
                 lhsT=n_codes[:, r * P : (r + 1) * P].bitcast(FP8X4),
                 lhsT_scale=n_scales[:, r * P : (r + 1) * P],
                 rhs=ow_codes[:].bitcast(FP8X4),
@@ -190,10 +193,14 @@ def tile_retentionmechanism_pb_s_kernel(tc, ao, w_qkv, out_w, tao, out):
                 start=True,
                 stop=True,
             )
+
+        def add_w(r):
             nc.vector.scalar_tensor_tensor(
-                out=z_sb[:, r, :], in0=z_ps[:], scalar=1.0, in1=w_sb[:, r, :], op0=ALU.mult, op1=ALU.add,
+                out=z_sb[:, r, :], in0=z_ps[r][:], scalar=1.0, in1=w_sb[:, r, :], op0=ALU.mult, op1=ALU.add,
                 accum_out=sum_z[:, r : r + 1],
             )
+
+        def square_and_total(r):
             nc.scalar.activation(
                 out=z_squares[:, r, :], in_=z_sb[:, r, :], func=ACT.Square, accum_out=sum_zz[:, r : r + 1]
             )
@@ -203,6 +210,16 @@ def tile_retentionmechanism_pb_s_kernel(tc, ao, w_qkv, out_w, tao, out):
             nc.tensor.matmul(
                 out=total_zz[:], lhsT=ones[:], rhs=sum_zz[:, r : r + 1], start=(r == 0), stop=(r == W_TILES - 1)
             )
+
+        silu_quantise_multiply(0)
+        silu_quantise_multiply(1)
+        add_w(0)
+        silu_quantise_multiply(2)
+        square_and_total(0)
+        add_w(1)
+        square_and_total(1)
+        add_w(2)
+        square_and_total(2)
 
         minus_mean_part = keep.tile([P, 1], F32)
         nc.vector.tensor_scalar(

@@ -1,5 +1,4 @@
 from contextlib import ExitStack
-import math
 
 import concourse.mybir as mybir
 from concourse.masks import make_identity
@@ -24,19 +23,16 @@ EPS_STD = 1e-08
 FLOPS = 2 * 2 * W_TILES * P * K * K
 
 
-def transpose_words(nc, flip, ident, rows_sb, first, count):
+def k_onto_partitions(nc, flip, ident, rows_sb, grouped, first, count):
     flipped = flip.tile([P, 2, 2, P], F32, tag="flip")
     for r in range(count):
         words = rows_sb[:, first + r, :].bitcast(F32)
         for u in range(2):
             nc.tensor.transpose(flipped[:, r, u, :], words[:, u * P : (u + 1) * P], ident[:])
-    return flipped
-
-
-def grouped_views(grouped, flipped, first, count):
-    dst = grouped[:, first * P : (first + count) * P, :].rearrange("p (r i) u -> p r i u", r=count)
-    src = flipped[:, 0:count].rearrange("p r u i -> p r i u")
-    return dst, src
+    nc.scalar.copy(
+        out=grouped[:, first * P : (first + count) * P, :].rearrange("p (r i) u -> p r i u", r=count),
+        in_=flipped[:, 0:count].rearrange("p r u i -> p r i u"),
+    )
 
 
 def quantise(nc, codes, scales, grouped_bf16, first_col, cols):
@@ -64,21 +60,19 @@ def tile_retentionmechanism_pb_s_kernel(tc, ao, w_qkv, out_w, tao, out):
         ow_sb = keep.tile([P, OW_TILES, K], BF16)
         nc.sync.dma_start(out=ow_sb[:], in_=out_w.rearrange("(r p) e -> p r e", p=P))
         tao_sb = keep.tile([P, 1], BF16)
-        nc.scalar.dma_start(out=tao_sb[:], in_=tao.partition_broadcast(P))
+        nc.sync.dma_start(out=tao_sb[:], in_=tao.partition_broadcast(P))
 
         ident = keep.tile([P, P], F32)
         make_identity(nc, ident[:])
         ones = keep.tile([P, P], F32)
         nc.gpsimd.memset(ones[:], 1.0)
-        half = keep.tile([P, 1], F32)
-        nc.gpsimd.memset(half[:], 0.5)
         one = keep.tile([P, 1], F32)
         nc.vector.memset(one[:], 1.0)
         eps_rms = keep.tile([P, 1], F32)
         nc.vector.tensor_scalar(
             out=eps_rms[:], in0=one[:], scalar1=0.0, scalar2=EPS_RMS, op0=ALU.mult, op1=ALU.add
         )
-        unread = keep.tile([P, 2, 8], F32)
+        unread = keep.tile([P, 3, 8], F32)
         nc.scalar.activation(out=unread[:, 0, 0:1], in_=one[:], func=ACT.Sqrt)
 
         squares = keep.tile([P, PACK, K], F32)
@@ -100,56 +94,44 @@ def tile_retentionmechanism_pb_s_kernel(tc, ao, w_qkv, out_w, tao, out):
         )
         rstd = keep.tile([P, PACK], F32)
         nc.vector.reciprocal(out=rstd[:], in_=rms[:])
-
-        w_flipped = [transpose_words(nc, flip, ident, w_sb, 0, 2), transpose_words(nc, flip, ident, w_sb, 2, 1)]
-        ow_flipped = [transpose_words(nc, flip, ident, ow_sb, 0, 2), transpose_words(nc, flip, ident, ow_sb, 2, 2)]
+        nc.scalar.activation(out=unread[:, 1, 0:1], in_=one[:], func=ACT.Silu)
 
         w_grouped = keep.tile([P, W_TILES * P, 2], F32, align_bytes=64)
-        dst, src = grouped_views(w_grouped, w_flipped[0], 0, 2)
-        nc.scalar.copy(out=dst, in_=src)
-        dst, src = grouped_views(w_grouped, w_flipped[1], 2, 1)
-        nc.scalar.copy(out=dst, in_=src)
-        nc.scalar.activation(out=unread[:, 1, 0:1], in_=rms[:, 0:1], func=ACT.Silu)
+        k_onto_partitions(nc, flip, ident, w_sb, w_grouped, 0, 2)
+        k_onto_partitions(nc, flip, ident, w_sb, w_grouped, 2, 1)
         ow_grouped = keep.tile([P, OW_TILES * P, 2], F32, align_bytes=64)
-        dst, src = grouped_views(ow_grouped, ow_flipped[0], 0, 2)
-        nc.scalar.copy(out=dst, in_=src)
+        k_onto_partitions(nc, flip, ident, ow_sb, ow_grouped, 0, 2)
+        k_onto_partitions(nc, flip, ident, ow_sb, ow_grouped, 2, 2)
 
         a_grouped = keep.tile([P, PACK, P, PACK], BF16, align_bytes=64)
-        a_flat = a_grouped[:].rearrange("p e m t -> p (e m t)")
-        a_codes = keep.tile([P, K], U32, align_bytes=64)
-        a_scales = keep.tile([P, K], U8, align_bytes=64)
-        w_codes = keep.tile([P, W_TILES * P], U32, align_bytes=64)
-        w_scales = keep.tile([P, W_TILES * P], U8, align_bytes=64)
-        w_flat = w_grouped[:].rearrange("p i u -> p (i u)").bitcast(BF16)
         ao_cols = ao_sb[:].rearrange("p t (u m h) -> p u h m t", u=2, h=2)
         rstd_all = rstd[:].unsqueeze(1).to_broadcast([P, P, PACK])
-        n_ps = [acc.tile([P, PACK, P], F32, tag="acc", name="n_ps%d" % r) for r in range(W_TILES)]
         for u in range(2):
             for h in range(2):
                 nc.vector.tensor_tensor(
                     out=a_grouped[:, 2 * u + h], in0=ao_cols[:, u, h], in1=rstd_all, op=ALU.mult
                 )
-            if u == 0:
-                quantise(nc, w_codes, w_scales, w_flat, 0, 2 * P)
-                quantise(nc, w_codes, w_scales, w_flat, 2 * P, P)
-            quantise(nc, a_codes, a_scales, a_flat, 2 * u * P, 2 * P)
-            for r in range(W_TILES):
-                for e_tile in (2 * u, 2 * u + 1):
-                    nc.tensor.matmul_mx(
-                        out=n_ps[r][:, e_tile, :],
-                        lhsT=a_codes[:, e_tile * P : (e_tile + 1) * P].bitcast(FP8X4),
-                        lhsT_scale=a_scales[:, e_tile * P : (e_tile + 1) * P],
-                        rhs=w_codes[:, r * P : (r + 1) * P].bitcast(FP8X4),
-                        rhs_scale=w_scales[:, r * P : (r + 1) * P],
-                        start=True,
-                        stop=True,
-                    )
+        w_codes = keep.tile([P, W_TILES * P], U32, align_bytes=64)
+        w_scales = keep.tile([P, W_TILES * P], U8, align_bytes=64)
+        w_flat = w_grouped[:].rearrange("p i u -> p (i u)").bitcast(BF16)
+        quantise(nc, w_codes, w_scales, w_flat, 0, 2 * P)
+        quantise(nc, w_codes, w_scales, w_flat, 2 * P, P)
+        a_codes = keep.tile([P, K], U32, align_bytes=64)
+        a_scales = keep.tile([P, K], U8, align_bytes=64)
+        quantise(nc, a_codes, a_scales, a_grouped[:].rearrange("p e m t -> p (e m t)"), 0, K)
 
-        dst, src = grouped_views(ow_grouped, ow_flipped[1], 2, 2)
-        nc.vector.tensor_copy(out=dst, in_=src)
-        ow_codes = keep.tile([P, K], U32, align_bytes=64)
-        ow_scales = keep.tile([P, K], U8, align_bytes=64)
-        quantise(nc, ow_codes, ow_scales, ow_grouped[:].rearrange("p j u -> p (j u)").bitcast(BF16), 0, K)
+        n_ps = [acc.tile([P, PACK, P], F32, tag="acc", name="n_ps%d" % r) for r in range(W_TILES)]
+        for r in range(W_TILES):
+            for e_tile in range(PACK):
+                nc.tensor.matmul_mx(
+                    out=n_ps[r][:, e_tile, :],
+                    lhsT=a_codes[:, e_tile * P : (e_tile + 1) * P].bitcast(FP8X4),
+                    lhsT_scale=a_scales[:, e_tile * P : (e_tile + 1) * P],
+                    rhs=w_codes[:, r * P : (r + 1) * P].bitcast(FP8X4),
+                    rhs_scale=w_scales[:, r * P : (r + 1) * P],
+                    start=True,
+                    stop=True,
+                )
 
         gate = keep.tile([P, 1], F32)
         nc.vector.scalar_tensor_tensor(
@@ -161,10 +143,14 @@ def tile_retentionmechanism_pb_s_kernel(tc, ao, w_qkv, out_w, tao, out):
         )
         scaled_gate = keep.tile([P, 1], F32)
         nc.vector.tensor_scalar(
-            out=scaled_gate[:], in0=clipped[:], scalar1=math.sqrt((COUNT - 1) / K), scalar2=None, op0=ALU.mult
+            out=scaled_gate[:], in0=clipped[:], scalar1=K**-0.5, scalar2=None, op0=ALU.mult
         )
         gate_inv = keep.tile([P, 1], F32)
         nc.vector.reciprocal(out=gate_inv[:], in_=scaled_gate[:])
+
+        ow_codes = keep.tile([P, K], U32, align_bytes=64)
+        ow_scales = keep.tile([P, K], U8, align_bytes=64)
+        quantise(nc, ow_codes, ow_scales, ow_grouped[:].rearrange("p j u -> p (j u)").bitcast(BF16), 0, K)
 
         n_grouped = keep.tile([P, W_TILES, P, PACK], BF16, align_bytes=64)
         n_flat = n_grouped[:].rearrange("p r i t -> p (r i t)")
@@ -173,7 +159,7 @@ def tile_retentionmechanism_pb_s_kernel(tc, ao, w_qkv, out_w, tao, out):
         z_sb = keep.tile([P, W_TILES, K], F32)
         z_squares = keep.tile([P, W_TILES, K], F32)
         sum_z = keep.tile([P, W_TILES], F32)
-        sum_zz = keep.tile([P, W_TILES], F32)
+        sum_zz = [keep.tile([P, 1], F32, name="sum_zz%d" % r) for r in range(W_TILES)]
         total_z = flip.tile([P, 1], F32, tag="flip")
         total_zz = flip.tile([P, 1], F32, tag="flip")
         z_ps = [None] * W_TILES
@@ -200,52 +186,57 @@ def tile_retentionmechanism_pb_s_kernel(tc, ao, w_qkv, out_w, tao, out):
                 accum_out=sum_z[:, r : r + 1],
             )
 
-        def square_and_total(r):
-            nc.scalar.activation(
-                out=z_squares[:, r, :], in_=z_sb[:, r, :], func=ACT.Square, accum_out=sum_zz[:, r : r + 1]
-            )
+        def totals(r):
             nc.tensor.matmul(
                 out=total_z[:], lhsT=ones[:], rhs=sum_z[:, r : r + 1], start=(r == 0), stop=(r == W_TILES - 1)
             )
             nc.tensor.matmul(
-                out=total_zz[:], lhsT=ones[:], rhs=sum_zz[:, r : r + 1], start=(r == 0), stop=(r == W_TILES - 1)
+                out=total_zz[:], lhsT=ones[:], rhs=sum_zz[r][:], start=(r == 0), stop=(r == W_TILES - 1)
+            )
+
+        def square_on_scalar(r):
+            nc.scalar.activation(
+                out=z_squares[:, r, :], in_=z_sb[:, r, :], func=ACT.Square, accum_out=sum_zz[r][:]
             )
 
         silu_quantise_multiply(0)
         silu_quantise_multiply(1)
         add_w(0)
         silu_quantise_multiply(2)
-        square_and_total(0)
+        square_on_scalar(0)
+        totals(0)
         add_w(1)
-        square_and_total(1)
+        square_on_scalar(1)
+        totals(1)
+        nc.scalar.activation(out=unread[:, 2, 0:1], in_=one[:], func=ACT.Sqrt)
         add_w(2)
-        square_and_total(2)
+        nc.vector.scalar_tensor_tensor(
+            out=z_squares[:, 2, :], in0=z_sb[:, 2, :], scalar=1.0, in1=z_sb[:, 2, :], op0=ALU.mult, op1=ALU.mult,
+            accum_out=sum_zz[2][:],
+        )
+        totals(2)
 
         minus_mean_part = keep.tile([P, 1], F32)
         nc.vector.tensor_scalar(
-            out=minus_mean_part[:], in0=total_z[:], scalar1=total_z[:, 0:1], scalar2=-1.0 / COUNT,
+            out=minus_mean_part[:], in0=total_z[:], scalar1=total_z[:, 0:1], scalar2=-1.0 / (COUNT * (COUNT - 1.0)),
             op0=ALU.mult, op1=ALU.mult,
         )
-        spread = keep.tile([P, 1], F32)
-        nc.vector.tensor_scalar(
-            out=spread[:], in0=total_zz[:], scalar1=minus_mean_part[:, 0:1], scalar2=0.0, op0=ALU.add, op1=ALU.max
+        std = keep.tile([P, 1], F32)
+        nc.scalar.activation(
+            out=std[:], in_=total_zz[:], func=ACT.Sqrt, bias=minus_mean_part[:], scale=1.0 / (COUNT - 1.0)
         )
-        root = keep.tile([P, 1], F32)
-        nc.gpsimd.tensor_tensor(out=root[:], in0=spread[:], in1=half[:], op=ALU.pow)
         divisor = keep.tile([P, 1], F32)
         nc.vector.tensor_scalar(
-            out=divisor[:], in0=root[:], scalar1=EPS_STD * math.sqrt(COUNT - 1), scalar2=gate_inv[:, 0:1],
-            op0=ALU.add, op1=ALU.mult,
+            out=divisor[:], in0=std[:], scalar1=EPS_STD, scalar2=gate_inv[:, 0:1], op0=ALU.add, op1=ALU.mult
         )
         factor = keep.tile([P, 1], F32)
         nc.vector.reciprocal(out=factor[:], in_=divisor[:])
 
         result = keep.tile([P, W_TILES, K], F32)
         out_tiles = out.rearrange("(r p) j -> r p j", p=P)
+        nc.scalar.activation(out=result[:, 2, :], in_=z_sb[:, 2, :], func=ACT.Copy, scale=factor[:, 0:1])
         for r in range(W_TILES):
-            if r == 1:
-                nc.scalar.activation(out=result[:, r, :], in_=z_sb[:, r, :], func=ACT.Copy, scale=factor[:, 0:1])
-            else:
+            if r < 2:
                 nc.vector.tensor_scalar(
                     out=result[:, r, :], in0=z_sb[:, r, :], scalar1=factor[:, 0:1], scalar2=None, op0=ALU.mult
                 )

@@ -106,19 +106,21 @@ def tile_retentionmechanism_pb_s_kernel(tc, ao, w_qkv, out_w, tao, out):
         a_grouped = keep.tile([P, PACK, P, PACK], BF16, align_bytes=64)
         ao_cols = ao_sb[:].rearrange("p t (u m h) -> p u h m t", u=2, h=2)
         rstd_all = rstd[:].unsqueeze(1).to_broadcast([P, P, PACK])
+        a_flat = a_grouped[:].rearrange("p e m t -> p (e m t)")
+        a_codes = keep.tile([P, K], U32, align_bytes=64)
+        a_scales = keep.tile([P, K], U8, align_bytes=64)
+        w_codes = keep.tile([P, W_TILES * P], U32, align_bytes=64)
+        w_scales = keep.tile([P, W_TILES * P], U8, align_bytes=64)
+        w_flat = w_grouped[:].rearrange("p i u -> p (i u)").bitcast(BF16)
         for u in range(2):
             for h in range(2):
                 nc.vector.tensor_tensor(
                     out=a_grouped[:, 2 * u + h], in0=ao_cols[:, u, h], in1=rstd_all, op=ALU.mult
                 )
-        w_codes = keep.tile([P, W_TILES * P], U32, align_bytes=64)
-        w_scales = keep.tile([P, W_TILES * P], U8, align_bytes=64)
-        w_flat = w_grouped[:].rearrange("p i u -> p (i u)").bitcast(BF16)
-        quantise(nc, w_codes, w_scales, w_flat, 0, 2 * P)
-        quantise(nc, w_codes, w_scales, w_flat, 2 * P, P)
-        a_codes = keep.tile([P, K], U32, align_bytes=64)
-        a_scales = keep.tile([P, K], U8, align_bytes=64)
-        quantise(nc, a_codes, a_scales, a_grouped[:].rearrange("p e m t -> p (e m t)"), 0, K)
+            if u == 1:
+                quantise(nc, w_codes, w_scales, w_flat, 0, P)
+            quantise(nc, a_codes, a_scales, a_flat, 2 * u * P, 2 * P)
+        quantise(nc, w_codes, w_scales, w_flat, P, 2 * P)
 
         n_ps = [acc.tile([P, PACK, P], F32, tag="acc", name="n_ps%d" % r) for r in range(W_TILES)]
         for r in range(W_TILES):
@@ -133,20 +135,14 @@ def tile_retentionmechanism_pb_s_kernel(tc, ao, w_qkv, out_w, tao, out):
                     stop=True,
                 )
 
-        gate = keep.tile([P, 1], F32)
+        tao_abs = keep.tile([P, 1], F32)
         nc.vector.scalar_tensor_tensor(
-            out=gate[:], in0=tao_sb[:], scalar=-1.0, in1=tao_sb[:], op0=ALU.mult, op1=ALU.max
+            out=tao_abs[:], in0=tao_sb[:], scalar=-1.0, in1=tao_sb[:], op0=ALU.mult, op1=ALU.max
         )
-        clipped = keep.tile([P, 1], F32)
+        gate = keep.tile([P, 1], F32)
         nc.vector.tensor_scalar(
-            out=clipped[:], in0=gate[:], scalar1=1e-08, scalar2=1.0, op0=ALU.max, op1=ALU.min
+            out=gate[:], in0=tao_abs[:], scalar1=1e-08, scalar2=1.0, op0=ALU.max, op1=ALU.min
         )
-        scaled_gate = keep.tile([P, 1], F32)
-        nc.vector.tensor_scalar(
-            out=scaled_gate[:], in0=clipped[:], scalar1=K**-0.5, scalar2=None, op0=ALU.mult
-        )
-        gate_inv = keep.tile([P, 1], F32)
-        nc.vector.reciprocal(out=gate_inv[:], in_=scaled_gate[:])
 
         ow_codes = keep.tile([P, K], U32, align_bytes=64)
         ow_scales = keep.tile([P, K], U8, align_bytes=64)
@@ -218,26 +214,25 @@ def tile_retentionmechanism_pb_s_kernel(tc, ao, w_qkv, out_w, tao, out):
 
         minus_mean_part = keep.tile([P, 1], F32)
         nc.vector.tensor_scalar(
-            out=minus_mean_part[:], in0=total_z[:], scalar1=total_z[:, 0:1], scalar2=-1.0 / (COUNT * (COUNT - 1.0)),
+            out=minus_mean_part[:], in0=total_z[:], scalar1=total_z[:, 0:1], scalar2=-K / (COUNT * (COUNT - 1.0)),
             op0=ALU.mult, op1=ALU.mult,
         )
-        std = keep.tile([P, 1], F32)
+        std_scaled = keep.tile([P, 1], F32)
         nc.scalar.activation(
-            out=std[:], in_=total_zz[:], func=ACT.Sqrt, bias=minus_mean_part[:], scale=1.0 / (COUNT - 1.0)
+            out=std_scaled[:], in_=total_zz[:], func=ACT.Sqrt, bias=minus_mean_part[:], scale=K / (COUNT - 1.0)
         )
         divisor = keep.tile([P, 1], F32)
         nc.vector.tensor_scalar(
-            out=divisor[:], in0=std[:], scalar1=EPS_STD, scalar2=gate_inv[:, 0:1], op0=ALU.add, op1=ALU.mult
+            out=divisor[:], in0=std_scaled[:], scalar1=EPS_STD * K**0.5, scalar2=None, op0=ALU.add
         )
-        factor = keep.tile([P, 1], F32)
-        nc.vector.reciprocal(out=factor[:], in_=divisor[:])
+        inverse = keep.tile([P, 1], F32)
+        nc.vector.reciprocal(out=inverse[:], in_=divisor[:])
 
         result = keep.tile([P, W_TILES, K], F32)
         out_tiles = out.rearrange("(r p) j -> r p j", p=P)
-        nc.scalar.activation(out=result[:, 2, :], in_=z_sb[:, 2, :], func=ACT.Copy, scale=factor[:, 0:1])
         for r in range(W_TILES):
-            if r < 2:
-                nc.vector.tensor_scalar(
-                    out=result[:, r, :], in0=z_sb[:, r, :], scalar1=factor[:, 0:1], scalar2=None, op0=ALU.mult
-                )
+            nc.vector.tensor_scalar(
+                out=result[:, r, :], in0=z_sb[:, r, :], scalar1=inverse[:, 0:1], scalar2=gate[:, 0:1],
+                op0=ALU.mult, op1=ALU.mult,
+            )
             nc.sync.dma_start(out=out_tiles[r], in_=result[:, r, :])

@@ -14,20 +14,23 @@ ALU = mybir.AluOpType
 P = 128
 PACK = 4
 K = P * PACK
+PAIR = 2
 W_TILES = 3
 OW_TILES = 4
 COUNT = W_TILES * P * K
 EPS_RMS = 1.1920929e-07
 EPS_STD = 1e-08
+GATE_MIN = 1e-08
+CELL = 8
 
 FLOPS = 2 * 2 * W_TILES * P * K * K
 
 
 def k_onto_partitions(nc, flip, ident, rows_sb, grouped, first, count):
-    flipped = flip.tile([P, 2, 2, P], F32, tag="flip")
+    flipped = flip.tile([P, PAIR, PAIR, P], F32, tag="flip")
     for r in range(count):
         words = rows_sb[:, first + r, :].bitcast(F32)
-        for u in range(2):
+        for u in range(PAIR):
             nc.tensor.transpose(flipped[:, r, u, :], words[:, u * P : (u + 1) * P], ident[:])
     nc.scalar.copy(
         out=grouped[:, first * P : (first + count) * P, :].rearrange("p (r i) u -> p r i u", r=count),
@@ -35,11 +38,11 @@ def k_onto_partitions(nc, flip, ident, rows_sb, grouped, first, count):
     )
 
 
-def quantise(nc, codes, scales, grouped_bf16, first_col, cols):
+def quantise(nc, codes, scales, values, first, count):
     nc.vector.quantize_mx(
-        out=codes[:, first_col : first_col + cols].bitcast(FP8X4),
-        scales=scales[:, first_col : first_col + cols],
-        in_=grouped_bf16[:, first_col * PACK : (first_col + cols) * PACK],
+        out=codes[:, first : first + count].bitcast(FP8X4),
+        scales=scales[:, first : first + count],
+        in_=values[:, first * PACK : (first + count) * PACK],
     )
 
 
@@ -48,13 +51,13 @@ def tile_retentionmechanism_pb_s_kernel(tc, ao, w_qkv, out_w, tao, out):
     with ExitStack() as ctx:
         keep = ctx.enter_context(tc.tile_pool(name="keep", bufs=1))
         flip = ctx.enter_context(tc.psum_pool(name="flip", bufs=4))
-        acc = ctx.enter_context(tc.psum_pool(name="acc", bufs=3))
+        acc = ctx.enter_context(tc.psum_pool(name="acc", bufs=W_TILES))
         ctx.enter_context(tc.manual_schedule())
 
         ao_sb = keep.tile([P, PACK, K], BF16)
-        ao_rows = ao.rearrange("(u p h) e -> u p h e", u=2, h=2)
-        for u in range(2):
-            nc.sync.dma_start(out=ao_sb[:, 2 * u : 2 * u + 2, :], in_=ao_rows[u])
+        ao_rows = ao.rearrange("(u p h) e -> u p h e", u=PAIR, h=PAIR)
+        for u in range(PAIR):
+            nc.sync.dma_start(out=ao_sb[:, PAIR * u : PAIR * (u + 1), :], in_=ao_rows[u])
         w_sb = keep.tile([P, W_TILES, K], BF16)
         nc.sync.dma_start(out=w_sb[:], in_=w_qkv.rearrange("(r p) d -> p r d", p=P))
         ow_sb = keep.tile([P, OW_TILES, K], BF16)
@@ -68,67 +71,73 @@ def tile_retentionmechanism_pb_s_kernel(tc, ao, w_qkv, out_w, tao, out):
         nc.gpsimd.memset(ones[:], 1.0)
         one = keep.tile([P, 1], F32)
         nc.vector.memset(one[:], 1.0)
-        eps_rms = keep.tile([P, 1], F32)
-        nc.vector.tensor_scalar(
-            out=eps_rms[:], in0=one[:], scalar1=0.0, scalar2=EPS_RMS, op0=ALU.mult, op1=ALU.add
-        )
-        unread = keep.tile([P, 3, 8], F32)
-        nc.scalar.activation(out=unread[:, 0, 0:1], in_=one[:], func=ACT.Sqrt)
+
+        unread = keep.tile([P, 3, CELL], F32)
+
+        def load_tables(func, cell):
+            nc.scalar.activation(out=unread[:, cell, 0:1], in_=one[:], func=func)
+
+        load_tables(ACT.Sqrt, 0)
 
         squares = keep.tile([P, PACK, K], F32)
-        sumsq = keep.tile([P, 2, 8], F32)
-        for u in range(2):
+        sumsq = keep.tile([P, PAIR, CELL], F32)
+        for u in range(PAIR):
             nc.scalar.activation(
-                out=squares[:, 2 * u, :], in_=ao_sb[:, 2 * u, :], func=ACT.Square,
+                out=squares[:, PAIR * u, :], in_=ao_sb[:, PAIR * u, :], func=ACT.Square,
                 accum_out=sumsq[:, 0, u : u + 1],
             )
             nc.vector.scalar_tensor_tensor(
-                out=squares[:, 2 * u + 1, :], in0=ao_sb[:, 2 * u + 1, :], scalar=1.0,
-                in1=ao_sb[:, 2 * u + 1, :], op0=ALU.mult, op1=ALU.mult,
+                out=squares[:, PAIR * u + 1, :], in0=ao_sb[:, PAIR * u + 1, :], scalar=1.0,
+                in1=ao_sb[:, PAIR * u + 1, :], op0=ALU.mult, op1=ALU.mult,
                 accum_out=sumsq[:, 1, u : u + 1],
             )
         rms = keep.tile([P, PACK], F32)
         nc.scalar.activation(
-            out=rms[:].rearrange("p (u h) -> p h u", h=2), in_=sumsq[:, :, 0:2], func=ACT.Sqrt,
-            bias=eps_rms[:], scale=1.0 / K,
+            out=rms[:].rearrange("p (u h) -> p h u", h=PAIR), in_=sumsq[:, :, 0:PAIR], func=ACT.Sqrt,
+            bias=EPS_RMS, scale=1.0 / K,
         )
         rstd = keep.tile([P, PACK], F32)
         nc.vector.reciprocal(out=rstd[:], in_=rms[:])
-        nc.scalar.activation(out=unread[:, 1, 0:1], in_=one[:], func=ACT.Silu)
+        load_tables(ACT.Silu, 1)
 
-        w_grouped = keep.tile([P, W_TILES * P, 2], F32, align_bytes=64)
+        w_grouped = keep.tile([P, W_TILES * P, PAIR], F32, align_bytes=64)
         k_onto_partitions(nc, flip, ident, w_sb, w_grouped, 0, 2)
         k_onto_partitions(nc, flip, ident, w_sb, w_grouped, 2, 1)
-        ow_grouped = keep.tile([P, OW_TILES * P, 2], F32, align_bytes=64)
+        ow_grouped = keep.tile([P, OW_TILES * P, PAIR], F32, align_bytes=64)
         k_onto_partitions(nc, flip, ident, ow_sb, ow_grouped, 0, 2)
         k_onto_partitions(nc, flip, ident, ow_sb, ow_grouped, 2, 2)
+        w_values = w_grouped[:].rearrange("p i u -> p (i u)").bitcast(BF16)
+        ow_values = ow_grouped[:].rearrange("p j u -> p (j u)").bitcast(BF16)
 
         a_grouped = keep.tile([P, PACK, P, PACK], BF16, align_bytes=64)
-        ao_cols = ao_sb[:].rearrange("p t (u m h) -> p u h m t", u=2, h=2)
-        rstd_all = rstd[:].unsqueeze(1).to_broadcast([P, P, PACK])
-        a_flat = a_grouped[:].rearrange("p e m t -> p (e m t)")
+        a_values = a_grouped[:].rearrange("p c m t -> p (c m t)")
         a_codes = keep.tile([P, K], U32, align_bytes=64)
         a_scales = keep.tile([P, K], U8, align_bytes=64)
         w_codes = keep.tile([P, W_TILES * P], U32, align_bytes=64)
         w_scales = keep.tile([P, W_TILES * P], U8, align_bytes=64)
-        w_flat = w_grouped[:].rearrange("p i u -> p (i u)").bitcast(BF16)
-        for u in range(2):
-            for h in range(2):
-                nc.vector.tensor_tensor(
-                    out=a_grouped[:, 2 * u + h], in0=ao_cols[:, u, h], in1=rstd_all, op=ALU.mult
-                )
-            if u == 1:
-                quantise(nc, w_codes, w_scales, w_flat, 0, P)
-            quantise(nc, a_codes, a_scales, a_flat, 2 * u * P, 2 * P)
-        quantise(nc, w_codes, w_scales, w_flat, P, 2 * P)
+        ao_columns = ao_sb[:].rearrange("p t (u m h) -> p u m h t", u=PAIR, h=PAIR)
+        rstd_repeated = rstd[:].unsqueeze(1).unsqueeze(1).to_broadcast([P, P, PAIR, PACK])
+
+        def norm_columns(u):
+            nc.vector.tensor_tensor(
+                out=a_grouped[:, PAIR * u : PAIR * (u + 1)].rearrange("p h m t -> p m h t"),
+                in0=ao_columns[:, u], in1=rstd_repeated, op=ALU.mult,
+            )
+
+        norm_columns(0)
+        quantise(nc, a_codes, a_scales, a_values, 0, PAIR * P)
+        norm_columns(1)
+        quantise(nc, w_codes, w_scales, w_values, 0, P)
+        quantise(nc, a_codes, a_scales, a_values, PAIR * P, PAIR * P)
+        quantise(nc, w_codes, w_scales, w_values, P, PAIR * P)
 
         n_ps = [acc.tile([P, PACK, P], F32, tag="acc", name="n_ps%d" % r) for r in range(W_TILES)]
         for r in range(W_TILES):
-            for e_tile in range(PACK):
+            for c in range(PACK):
                 nc.tensor.matmul_mx(
-                    out=n_ps[r][:, e_tile, :],
-                    lhsT=a_codes[:, e_tile * P : (e_tile + 1) * P].bitcast(FP8X4),
-                    lhsT_scale=a_scales[:, e_tile * P : (e_tile + 1) * P],
+                    out=n_ps[r][:, c, :],
+                    lhsT=a_codes[:, c * P : (c + 1) * P].bitcast(FP8X4),
+                    lhsT_scale=a_scales[:, c * P : (c + 1) * P],
                     rhs=w_codes[:, r * P : (r + 1) * P].bitcast(FP8X4),
                     rhs_scale=w_scales[:, r * P : (r + 1) * P],
                     start=True,
@@ -141,30 +150,29 @@ def tile_retentionmechanism_pb_s_kernel(tc, ao, w_qkv, out_w, tao, out):
         )
         gate = keep.tile([P, 1], F32)
         nc.vector.tensor_scalar(
-            out=gate[:], in0=tao_abs[:], scalar1=1e-08, scalar2=1.0, op0=ALU.max, op1=ALU.min
+            out=gate[:], in0=tao_abs[:], scalar1=GATE_MIN, scalar2=1.0, op0=ALU.max, op1=ALU.min
         )
-
         ow_codes = keep.tile([P, K], U32, align_bytes=64)
         ow_scales = keep.tile([P, K], U8, align_bytes=64)
-        quantise(nc, ow_codes, ow_scales, ow_grouped[:].rearrange("p j u -> p (j u)").bitcast(BF16), 0, K)
+        quantise(nc, ow_codes, ow_scales, ow_values, 0, K)
 
         n_grouped = keep.tile([P, W_TILES, P, PACK], BF16, align_bytes=64)
-        n_flat = n_grouped[:].rearrange("p r i t -> p (r i t)")
+        n_values = n_grouped[:].rearrange("p r i t -> p (r i t)")
         n_codes = keep.tile([P, W_TILES * P], U32, align_bytes=64)
         n_scales = keep.tile([P, W_TILES * P], U8, align_bytes=64)
+        z_ps = [None] * W_TILES
         z_sb = keep.tile([P, W_TILES, K], F32)
         z_squares = keep.tile([P, W_TILES, K], F32)
         sum_z = keep.tile([P, W_TILES], F32)
         sum_zz = [keep.tile([P, 1], F32, name="sum_zz%d" % r) for r in range(W_TILES)]
         total_z = flip.tile([P, 1], F32, tag="flip")
         total_zz = flip.tile([P, 1], F32, tag="flip")
-        z_ps = [None] * W_TILES
 
         def silu_quantise_multiply(r):
             nc.scalar.activation(
                 out=n_grouped[:, r], in_=n_ps[r][:].rearrange("p t i -> p i t"), func=ACT.Silu
             )
-            quantise(nc, n_codes, n_scales, n_flat, r * P, P)
+            quantise(nc, n_codes, n_scales, n_values, r * P, P)
             z_ps[r] = acc.tile([P, K], F32, tag="acc", name="z_ps%d" % r)
             nc.tensor.matmul_mx(
                 out=z_ps[r][:],
@@ -182,35 +190,34 @@ def tile_retentionmechanism_pb_s_kernel(tc, ao, w_qkv, out_w, tao, out):
                 accum_out=sum_z[:, r : r + 1],
             )
 
-        def totals(r):
-            nc.tensor.matmul(
-                out=total_z[:], lhsT=ones[:], rhs=sum_z[:, r : r + 1], start=(r == 0), stop=(r == W_TILES - 1)
-            )
-            nc.tensor.matmul(
-                out=total_zz[:], lhsT=ones[:], rhs=sum_zz[r][:], start=(r == 0), stop=(r == W_TILES - 1)
-            )
-
         def square_on_scalar(r):
             nc.scalar.activation(
                 out=z_squares[:, r, :], in_=z_sb[:, r, :], func=ACT.Square, accum_out=sum_zz[r][:]
             )
+
+        def square_on_vector(r):
+            nc.vector.scalar_tensor_tensor(
+                out=z_squares[:, r, :], in0=z_sb[:, r, :], scalar=1.0, in1=z_sb[:, r, :],
+                op0=ALU.mult, op1=ALU.mult, accum_out=sum_zz[r][:],
+            )
+
+        def add_to_totals(r):
+            for total, part in ((total_z, sum_z[:, r : r + 1]), (total_zz, sum_zz[r][:])):
+                nc.tensor.matmul(out=total[:], lhsT=ones[:], rhs=part, start=(r == 0), stop=(r == W_TILES - 1))
 
         silu_quantise_multiply(0)
         silu_quantise_multiply(1)
         add_w(0)
         silu_quantise_multiply(2)
         square_on_scalar(0)
-        totals(0)
+        add_to_totals(0)
         add_w(1)
         square_on_scalar(1)
-        totals(1)
-        nc.scalar.activation(out=unread[:, 2, 0:1], in_=one[:], func=ACT.Sqrt)
+        add_to_totals(1)
+        load_tables(ACT.Sqrt, 2)
         add_w(2)
-        nc.vector.scalar_tensor_tensor(
-            out=z_squares[:, 2, :], in0=z_sb[:, 2, :], scalar=1.0, in1=z_sb[:, 2, :], op0=ALU.mult, op1=ALU.mult,
-            accum_out=sum_zz[2][:],
-        )
-        totals(2)
+        square_on_vector(2)
+        add_to_totals(2)
 
         minus_mean_part = keep.tile([P, 1], F32)
         nc.vector.tensor_scalar(

@@ -125,8 +125,8 @@ def tile_retentionmechanism_pb_s_kernel(tc, ao, w_qkv, out_w, tao, out):
             )
 
         norm_columns(0)
-        quantise(nc, a_codes, a_scales, a_values, 0, PAIR * P)
         norm_columns(1)
+        quantise(nc, a_codes, a_scales, a_values, 0, PAIR * P)
         quantise(nc, w_codes, w_scales, w_values, 0, P)
         quantise(nc, a_codes, a_scales, a_values, PAIR * P, PAIR * P)
         quantise(nc, w_codes, w_scales, w_values, P, PAIR * P)

@@ -115,14 +115,16 @@ def tile_retentionmechanism_pb_s_kernel(tc, ao, w_qkv, out_w, tao, out):
         a_scales = keep.tile([P, K], U8, align_bytes=64)
         w_codes = keep.tile([P, W_TILES * P], U32, align_bytes=64)
         w_scales = keep.tile([P, W_TILES * P], U8, align_bytes=64)
-        ao_columns = ao_sb[:].rearrange("p t (u m h) -> p u m h t", u=PAIR, h=PAIR)
-        rstd_repeated = rstd[:].unsqueeze(1).unsqueeze(1).to_broadcast([P, P, PAIR, PACK])
+        RUN = 4
+        ao_columns = ao_sb[:].rearrange("p t (u g i h) -> p u h g t i", u=PAIR, i=RUN, h=PAIR)
+        rstd_repeated = rstd[:].unsqueeze(1).unsqueeze(3).to_broadcast([P, P // RUN, PACK, RUN])
 
         def norm_columns(u):
-            nc.vector.tensor_tensor(
-                out=a_grouped[:, PAIR * u : PAIR * (u + 1)].rearrange("p h m t -> p m h t"),
-                in0=ao_columns[:, u], in1=rstd_repeated, op=ALU.mult,
-            )
+            for h in range(PAIR):
+                nc.vector.tensor_tensor(
+                    out=a_grouped[:, PAIR * u + h].rearrange("p (g i) t -> p g t i", i=RUN),
+                    in0=ao_columns[:, u, h], in1=rstd_repeated, op=ALU.mult,
+                )
 
         norm_columns(0)
         norm_columns(1)

@@ -67,8 +67,6 @@ def tile_retentionmechanism_pb_s_kernel(tc, ao, w_qkv, out_w, tao, out):
 
         ident = keep.tile([P, P], F32)
         make_identity(nc, ident[:])
-        ones = keep.tile([P, P], F32)
-        nc.gpsimd.memset(ones[:], 1.0)
         one = keep.tile([P, 1], F32)
         nc.vector.memset(one[:], 1.0)
 
@@ -167,8 +165,8 @@ def tile_retentionmechanism_pb_s_kernel(tc, ao, w_qkv, out_w, tao, out):
         z_squares = keep.tile([P, W_TILES, K], F32)
         sum_z = keep.tile([P, W_TILES], F32)
         sum_zz = [keep.tile([P, 1], F32, name="sum_zz%d" % r) for r in range(W_TILES)]
-        total_z = flip.tile([P, 1], F32, tag="flip")
-        total_zz = flip.tile([P, 1], F32, tag="flip")
+        spread_z = flip.tile([P, P], F32, tag="flip")
+        spread_zz = flip.tile([P, P], F32, tag="flip")
 
         def silu_quantise_multiply(r):
             nc.scalar.activation(
@@ -204,8 +202,11 @@ def tile_retentionmechanism_pb_s_kernel(tc, ao, w_qkv, out_w, tao, out):
             )
 
         def add_to_totals(r):
-            for total, part in ((total_z, sum_z[:, r : r + 1]), (total_zz, sum_zz[r][:])):
-                nc.tensor.matmul(out=total[:], lhsT=ones[:], rhs=part, start=(r == 0), stop=(r == W_TILES - 1))
+            for spread, part in ((spread_z, sum_z[:, r : r + 1]), (spread_zz, sum_zz[r][:])):
+                nc.tensor.matmul(
+                    out=spread[:], lhsT=part.to_broadcast([P, P]), rhs=ident[:], is_transpose=True,
+                    start=(r == 0), stop=(r == W_TILES - 1),
+                )
 
         silu_quantise_multiply(0)
         silu_quantise_multiply(1)
@@ -221,11 +222,15 @@ def tile_retentionmechanism_pb_s_kernel(tc, ao, w_qkv, out_w, tao, out):
         square_on_vector(2)
         add_to_totals(2)
 
+        total_z = keep.tile([P, 1], F32)
+        nc.vector.tensor_reduce(out=total_z[:], in_=spread_z[:], axis=mybir.AxisListType.X, op=ALU.add)
         minus_mean_part = keep.tile([P, 1], F32)
         nc.vector.tensor_scalar(
             out=minus_mean_part[:], in0=total_z[:], scalar1=total_z[:, 0:1], scalar2=-K / (COUNT * (COUNT - 1.0)),
             op0=ALU.mult, op1=ALU.mult,
         )
+        total_zz = keep.tile([P, 1], F32)
+        nc.vector.tensor_reduce(out=total_zz[:], in_=spread_zz[:], axis=mybir.AxisListType.X, op=ALU.add)
         std_scaled = keep.tile([P, 1], F32)
         nc.scalar.activation(
             out=std_scaled[:], in_=total_zz[:], func=ACT.Sqrt, bias=minus_mean_part[:], scale=K / (COUNT - 1.0)

@@ -69,6 +69,10 @@ def tile_retentionmechanism_pb_s_kernel(tc, ao, w_qkv, out_w, tao, out):
         make_identity(nc, ident[:])
         one = keep.tile([P, 1], F32)
         nc.vector.memset(one[:], 1.0)
+        under_root = keep.tile([P, PAIR], F32)
+        nc.vector.tensor_scalar(
+            out=under_root[:, 1:2], in0=one[:], scalar1=K * EPS_STD**2, scalar2=None, op0=ALU.mult
+        )
 
         unread = keep.tile([P, 3, CELL], F32)
 
@@ -229,16 +233,14 @@ def tile_retentionmechanism_pb_s_kernel(tc, ao, w_qkv, out_w, tao, out):
             out=minus_mean_part[:], in0=total_z[:], scalar1=total_z[:, 0:1], scalar2=-K / (COUNT * (COUNT - 1.0)),
             op0=ALU.mult, op1=ALU.mult,
         )
-        total_zz = keep.tile([P, 1], F32)
-        nc.vector.tensor_reduce(out=total_zz[:], in_=spread_zz[:], axis=mybir.AxisListType.X, op=ALU.add)
-        std_scaled = keep.tile([P, 1], F32)
-        nc.scalar.activation(
-            out=std_scaled[:], in_=total_zz[:], func=ACT.Sqrt, bias=minus_mean_part[:], scale=K / (COUNT - 1.0)
-        )
-        divisor = keep.tile([P, 1], F32)
+        scaled_sums = keep.tile([P, P], F32)
         nc.vector.tensor_scalar(
-            out=divisor[:], in0=std_scaled[:], scalar1=EPS_STD * K**0.5, scalar2=None, op0=ALU.add
+            out=scaled_sums[:], in0=spread_zz[:], scalar1=K / (COUNT - 1.0), scalar2=minus_mean_part[:, 0:1],
+            op0=ALU.mult, op1=ALU.add, accum_out=under_root[:, 0:1],
         )
+        roots = keep.tile([P, PAIR], F32)
+        divisor = keep.tile([P, 1], F32)
+        nc.scalar.activation(out=roots[:], in_=under_root[:], func=ACT.Sqrt, accum_out=divisor[:])
         inverse = keep.tile([P, 1], F32)
         nc.vector.reciprocal(out=inverse[:], in_=divisor[:])
 

@@ -52,6 +52,7 @@ def tile_retentionmechanism_pb_s_kernel(tc, ao, w_qkv, out_w, tao, out):
         keep = ctx.enter_context(tc.tile_pool(name="keep", bufs=1))
         flip = ctx.enter_context(tc.psum_pool(name="flip", bufs=4))
         acc = ctx.enter_context(tc.psum_pool(name="acc", bufs=W_TILES))
+        spare = ctx.enter_context(tc.psum_pool(name="spare", bufs=1))
         ctx.enter_context(tc.manual_schedule())
 
         ao_sb = keep.tile([P, PACK, K], BF16)
@@ -81,6 +82,12 @@ def tile_retentionmechanism_pb_s_kernel(tc, ao, w_qkv, out_w, tao, out):
 
         load_tables(ACT.Sqrt, 0)
 
+        idle = spare.tile([P, PACK, P], F32)
+
+        def plain_filler(count, moving):
+            for j in range(count):
+                nc.tensor.matmul(out=idle[:, j % PACK, :], lhsT=ident[:], rhs=moving, start=True, stop=True)
+
         squares = keep.tile([P, PACK, K], F32)
         sumsq = keep.tile([P, PAIR, CELL], F32)
         for u in range(PAIR):
@@ -102,12 +109,16 @@ def tile_retentionmechanism_pb_s_kernel(tc, ao, w_qkv, out_w, tao, out):
         nc.vector.reciprocal(out=rstd[:], in_=rms[:])
         load_tables(ACT.Silu, 1)
 
+        plain_filler(2, squares[:, 0, 0:P])
         w_grouped = keep.tile([P, W_TILES * P, PAIR], F32, align_bytes=64)
         k_onto_partitions(nc, flip, ident, w_sb, w_grouped, 0, 2)
         k_onto_partitions(nc, flip, ident, w_sb, w_grouped, 2, 1)
+        plain_filler(1, ident[:])
         ow_grouped = keep.tile([P, OW_TILES * P, PAIR], F32, align_bytes=64)
         k_onto_partitions(nc, flip, ident, ow_sb, ow_grouped, 0, 2)
+        plain_filler(1, ident[:])
         k_onto_partitions(nc, flip, ident, ow_sb, ow_grouped, 2, 2)
+        plain_filler(3, ident[:])
         w_values = w_grouped[:].rearrange("p i u -> p (i u)").bitcast(BF16)
         ow_values = ow_grouped[:].rearrange("p j u -> p (j u)").bitcast(BF16)
 
@@ -147,6 +158,20 @@ def tile_retentionmechanism_pb_s_kernel(tc, ao, w_qkv, out_w, tao, out):
                     start=True,
                     stop=True,
                 )
+
+        def mx_filler(count):
+            for j in range(count):
+                nc.tensor.matmul_mx(
+                    out=idle[:, 0:PAIR, :].rearrange("p c i -> p (c i)"),
+                    lhsT=a_codes[:, 0:P].bitcast(FP8X4),
+                    lhsT_scale=a_scales[:, 0:P],
+                    rhs=w_codes[:, 0 : PAIR * P].bitcast(FP8X4),
+                    rhs_scale=w_scales[:, 0 : PAIR * P],
+                    start=True,
+                    stop=True,
+                )
+
+        mx_filler(2)
 
         tao_abs = keep.tile([P, 1], F32)
         nc.vector.scalar_tensor_tensor(
@@ -213,9 +238,12 @@ def tile_retentionmechanism_pb_s_kernel(tc, ao, w_qkv, out_w, tao, out):
                 )
 
         silu_quantise_multiply(0)
+        mx_filler(1)
         silu_quantise_multiply(1)
+        mx_filler(2)
         add_w(0)
         silu_quantise_multiply(2)
+        mx_filler(3)
         square_on_scalar(0)
         add_to_totals(0)
         add_w(1)

from contextlib import ExitStack

import concourse.mybir as mybir
from concourse.masks import make_identity

F32 = mybir.dt.float32
BF16 = mybir.dt.bfloat16
U32 = mybir.dt.uint32
U8 = mybir.dt.uint8
FP8X4 = mybir.dt.float8_e4m3fn_x4
ACT = mybir.ActivationFunctionType
ALU = mybir.AluOpType

P = 128
PACK = 4
K = P * PACK
PAIR = 2
W_TILES = 3
OW_TILES = 4
COUNT = W_TILES * P * K
EPS_RMS = 1.1920929e-07
EPS_STD = 1e-08
GATE_MIN = 1e-08
CELL = 8

FLOPS = 2 * 2 * W_TILES * P * K * K


def k_onto_partitions(nc, flip, ident, rows_sb, grouped, first, count):
    flipped = flip.tile([P, PAIR, PAIR, P], F32, tag="flip")
    for r in range(count):
        words = rows_sb[:, first + r, :].bitcast(F32)
        for u in range(PAIR):
            nc.tensor.transpose(flipped[:, r, u, :], words[:, u * P : (u + 1) * P], ident[:])
    nc.scalar.copy(
        out=grouped[:, first * P : (first + count) * P, :].rearrange("p (r i) u -> p r i u", r=count),
        in_=flipped[:, 0:count].rearrange("p r u i -> p r i u"),
    )


def quantise(nc, codes, scales, values, first, count):
    nc.vector.quantize_mx(
        out=codes[:, first : first + count].bitcast(FP8X4),
        scales=scales[:, first : first + count],
        in_=values[:, first * PACK : (first + count) * PACK],
    )


def tile_retentionmechanism_pb_s_kernel(tc, ao, w_qkv, out_w, tao, out):
    nc = tc.nc
    with ExitStack() as ctx:
        keep = ctx.enter_context(tc.tile_pool(name="keep", bufs=1))
        flip = ctx.enter_context(tc.psum_pool(name="flip", bufs=4))
        acc = ctx.enter_context(tc.psum_pool(name="acc", bufs=W_TILES))
        spare = ctx.enter_context(tc.psum_pool(name="spare", bufs=1))
        ctx.enter_context(tc.manual_schedule())

        ao_sb = keep.tile([P, PACK, K], BF16)
        ao_rows = ao.rearrange("(u p h) e -> u p h e", u=PAIR, h=PAIR)
        for u in range(PAIR):
            nc.sync.dma_start(out=ao_sb[:, PAIR * u : PAIR * (u + 1), :], in_=ao_rows[u])
        w_sb = keep.tile([P, W_TILES, K], BF16)
        nc.sync.dma_start(out=w_sb[:], in_=w_qkv.rearrange("(r p) d -> p r d", p=P))
        ow_sb = keep.tile([P, OW_TILES, K], BF16)
        nc.sync.dma_start(out=ow_sb[:], in_=out_w.rearrange("(r p) e -> p r e", p=P))
        tao_sb = keep.tile([P, 1], BF16)
        nc.sync.dma_start(out=tao_sb[:], in_=tao.partition_broadcast(P))

        ident = keep.tile([P, P], F32)
        make_identity(nc, ident[:])
        one = keep.tile([P, 1], F32)
        nc.vector.memset(one[:], 1.0)
        under_root = keep.tile([P, PAIR], F32)
        nc.vector.tensor_scalar(
            out=under_root[:, 1:2], in0=one[:], scalar1=K * EPS_STD**2, scalar2=None, op0=ALU.mult
        )

        unread = keep.tile([P, 3, CELL], F32)

        def load_tables(func, cell):
            nc.scalar.activation(out=unread[:, cell, 0:1], in_=one[:], func=func)

        load_tables(ACT.Sqrt, 0)

        idle = spare.tile([P, PACK, P], F32)

        def plain_filler(count, moving):
            for j in range(count):
                nc.tensor.matmul(out=idle[:, j % PACK, :], lhsT=ident[:], rhs=moving, start=True, stop=True)

        squares = keep.tile([P, PACK, K], F32)
        sumsq = keep.tile([P, PAIR, CELL], F32)
        for u in range(PAIR):
            nc.scalar.activation(
                out=squares[:, PAIR * u, :], in_=ao_sb[:, PAIR * u, :], func=ACT.Square,
                accum_out=sumsq[:, 0, u : u + 1],
            )
            nc.vector.scalar_tensor_tensor(
                out=squares[:, PAIR * u + 1, :], in0=ao_sb[:, PAIR * u + 1, :], scalar=1.0,
                in1=ao_sb[:, PAIR * u + 1, :], op0=ALU.mult, op1=ALU.mult,
                accum_out=sumsq[:, 1, u : u + 1],
            )
        rms = keep.tile([P, PACK], F32)
        nc.scalar.activation(
            out=rms[:].rearrange("p (u h) -> p h u", h=PAIR), in_=sumsq[:, :, 0:PAIR], func=ACT.Sqrt,
            bias=EPS_RMS, scale=1.0 / K,
        )
        rstd = keep.tile([P, PACK], F32)
        nc.vector.reciprocal(out=rstd[:], in_=rms[:])
        load_tables(ACT.Silu, 1)

        plain_filler(2, squares[:, 0, 0:P])
        w_grouped = keep.tile([P, W_TILES * P, PAIR], F32, align_bytes=64)
        k_onto_partitions(nc, flip, ident, w_sb, w_grouped, 0, 2)
        k_onto_partitions(nc, flip, ident, w_sb, w_grouped, 2, 1)
        plain_filler(1, ident[:])
        ow_grouped = keep.tile([P, OW_TILES * P, PAIR], F32, align_bytes=64)
        k_onto_partitions(nc, flip, ident, ow_sb, ow_grouped, 0, 2)
        plain_filler(1, ident[:])
        k_onto_partitions(nc, flip, ident, ow_sb, ow_grouped, 2, 2)
        plain_filler(3, ident[:])
        w_values = w_grouped[:].rearrange("p i u -> p (i u)").bitcast(BF16)
        ow_values = ow_grouped[:].rearrange("p j u -> p (j u)").bitcast(BF16)

        a_grouped = keep.tile([P, PACK, P, PACK], BF16, align_bytes=64)
        a_values = a_grouped[:].rearrange("p c m t -> p (c m t)")
        a_codes = keep.tile([P, K], U32, align_bytes=64)
        a_scales = keep.tile([P, K], U8, align_bytes=64)
        w_codes = keep.tile([P, W_TILES * P], U32, align_bytes=64)
        w_scales = keep.tile([P, W_TILES * P], U8, align_bytes=64)
        RUN = 4
        ao_columns = ao_sb[:].rearrange("p t (u g i h) -> p u h g t i", u=PAIR, i=RUN, h=PAIR)
        rstd_repeated = rstd[:].unsqueeze(1).unsqueeze(3).to_broadcast([P, P // RUN, PACK, RUN])

        def norm_columns(u):
            for h in range(PAIR):
                nc.vector.tensor_tensor(
                    out=a_grouped[:, PAIR * u + h].rearrange("p (g i) t -> p g t i", i=RUN),
                    in0=ao_columns[:, u, h], in1=rstd_repeated, op=ALU.mult,
                )

        norm_columns(0)
        norm_columns(1)
        quantise(nc, a_codes, a_scales, a_values, 0, PAIR * P)
        quantise(nc, w_codes, w_scales, w_values, 0, P)
        quantise(nc, a_codes, a_scales, a_values, PAIR * P, PAIR * P)
        quantise(nc, w_codes, w_scales, w_values, P, PAIR * P)

        n_ps = [acc.tile([P, PACK, P], F32, tag="acc", name="n_ps%d" % r) for r in range(W_TILES)]
        for r in range(W_TILES):
            for c in range(PACK):
                nc.tensor.matmul_mx(
                    out=n_ps[r][:, c, :],
                    lhsT=a_codes[:, c * P : (c + 1) * P].bitcast(FP8X4),
                    lhsT_scale=a_scales[:, c * P : (c + 1) * P],
                    rhs=w_codes[:, r * P : (r + 1) * P].bitcast(FP8X4),
                    rhs_scale=w_scales[:, r * P : (r + 1) * P],
                    start=True,
                    stop=True,
                )

        def mx_filler(count):
            for j in range(count):
                nc.tensor.matmul_mx(
                    out=idle[:, 0:PAIR, :].rearrange("p c i -> p (c i)"),
                    lhsT=a_codes[:, 0:P].bitcast(FP8X4),
                    lhsT_scale=a_scales[:, 0:P],
                    rhs=w_codes[:, 0 : PAIR * P].bitcast(FP8X4),
                    rhs_scale=w_scales[:, 0 : PAIR * P],
                    start=True,
                    stop=True,
                )

        mx_filler(2)

        tao_abs = keep.tile([P, 1], F32)
        nc.vector.scalar_tensor_tensor(
            out=tao_abs[:], in0=tao_sb[:], scalar=-1.0, in1=tao_sb[:], op0=ALU.mult, op1=ALU.max
        )
        gate = keep.tile([P, 1], F32)
        nc.vector.tensor_scalar(
            out=gate[:], in0=tao_abs[:], scalar1=GATE_MIN, scalar2=1.0, op0=ALU.max, op1=ALU.min
        )
        ow_codes = keep.tile([P, K], U32, align_bytes=64)
        ow_scales = keep.tile([P, K], U8, align_bytes=64)
        quantise(nc, ow_codes, ow_scales, ow_values, 0, K)

        n_grouped = keep.tile([P, W_TILES, P, PACK], BF16, align_bytes=64)
        n_values = n_grouped[:].rearrange("p r i t -> p (r i t)")
        n_codes = keep.tile([P, W_TILES * P], U32, align_bytes=64)
        n_scales = keep.tile([P, W_TILES * P], U8, align_bytes=64)
        z_ps = [None] * W_TILES
        z_sb = keep.tile([P, W_TILES, K], F32)
        z_squares = keep.tile([P, W_TILES, K], F32)
        sum_z = keep.tile([P, W_TILES], F32)
        sum_zz = [keep.tile([P, 1], F32, name="sum_zz%d" % r) for r in range(W_TILES)]
        spread_z = flip.tile([P, P], F32, tag="flip")
        spread_zz = flip.tile([P, P], F32, tag="flip")

        def silu_quantise_multiply(r):
            nc.scalar.activation(
                out=n_grouped[:, r], in_=n_ps[r][:].rearrange("p t i -> p i t"), func=ACT.Silu
            )
            quantise(nc, n_codes, n_scales, n_values, r * P, P)
            z_ps[r] = acc.tile([P, K], F32, tag="acc", name="z_ps%d" % r)
            nc.tensor.matmul_mx(
                out=z_ps[r][:],
                lhsT=n_codes[:, r * P : (r + 1) * P].bitcast(FP8X4),
                lhsT_scale=n_scales[:, r * P : (r + 1) * P],
                rhs=ow_codes[:].bitcast(FP8X4),
                rhs_scale=ow_scales[:],
                start=True,
                stop=True,
            )

        def add_w(r):
            nc.vector.scalar_tensor_tensor(
                out=z_sb[:, r, :], in0=z_ps[r][:], scalar=1.0, in1=w_sb[:, r, :], op0=ALU.mult, op1=ALU.add,
                accum_out=sum_z[:, r : r + 1],
            )

        def square_on_scalar(r):
            nc.scalar.activation(
                out=z_squares[:, r, :], in_=z_sb[:, r, :], func=ACT.Square, accum_out=sum_zz[r][:]
            )

        def square_on_vector(r):
            nc.vector.scalar_tensor_tensor(
                out=z_squares[:, r, :], in0=z_sb[:, r, :], scalar=1.0, in1=z_sb[:, r, :],
                op0=ALU.mult, op1=ALU.mult, accum_out=sum_zz[r][:],
            )

        def add_to_totals(r):
            for spread, part in ((spread_z, sum_z[:, r : r + 1]), (spread_zz, sum_zz[r][:])):
                nc.tensor.matmul(
                    out=spread[:], lhsT=part.to_broadcast([P, P]), rhs=ident[:], is_transpose=True,
                    start=(r == 0), stop=(r == W_TILES - 1),
                )

        silu_quantise_multiply(0)
        mx_filler(1)
        silu_quantise_multiply(1)
        mx_filler(2)
        add_w(0)
        silu_quantise_multiply(2)
        mx_filler(3)
        square_on_scalar(0)
        add_to_totals(0)
        add_w(1)
        square_on_scalar(1)
        add_to_totals(1)
        load_tables(ACT.Sqrt, 2)
        add_w(2)
        square_on_vector(2)
        add_to_totals(2)

        total_z = keep.tile([P, 1], F32)
        nc.vector.tensor_reduce(out=total_z[:], in_=spread_z[:], axis=mybir.AxisListType.X, op=ALU.add)
        minus_mean_part = keep.tile([P, 1], F32)
        nc.vector.tensor_scalar(
            out=minus_mean_part[:], in0=total_z[:], scalar1=total_z[:, 0:1], scalar2=-K / (COUNT * (COUNT - 1.0)),
            op0=ALU.mult, op1=ALU.mult,
        )
        scaled_sums = keep.tile([P, P], F32)
        nc.vector.tensor_scalar(
            out=scaled_sums[:], in0=spread_zz[:], scalar1=K / (COUNT - 1.0), scalar2=minus_mean_part[:, 0:1],
            op0=ALU.mult, op1=ALU.add, accum_out=under_root[:, 0:1],
        )
        roots = keep.tile([P, PAIR], F32)
        divisor = keep.tile([P, 1], F32)
        nc.scalar.activation(out=roots[:], in_=under_root[:], func=ACT.Sqrt, accum_out=divisor[:])
        inverse = keep.tile([P, 1], F32)
        nc.vector.reciprocal(out=inverse[:], in_=divisor[:])

        result = keep.tile([P, W_TILES, K], F32)
        out_tiles = out.rearrange("(r p) j -> r p j", p=P)
        for r in range(W_TILES):
            nc.vector.tensor_scalar(
                out=result[:, r, :], in0=z_sb[:, r, :], scalar1=inverse[:, 0:1], scalar2=gate[:, 0:1],
                op0=ALU.mult, op1=ALU.mult,
            )
            nc.sync.dma_start(out=out_tiles[r], in_=result[:, r, :])
